import numpy as np
import ml_dtypes


def mxq(x, axis, fmt="e4m3"):
    dtype, down = {"e4m3": (ml_dtypes.float8_e4m3fn, 7), "e5m2": (ml_dtypes.float8_e5m2, 14)}[fmt]
    v = np.moveaxis(np.asarray(x, np.float32).astype(ml_dtypes.bfloat16).astype(np.float64), axis, -1)
    blocks = v.reshape(v.shape[:-1] + (-1, 32))
    amax = np.abs(blocks).max(-1, keepdims=True)
    byte = np.maximum(np.where(amax > 0, np.frexp(amax)[1] - 1 + 127, 0) - down, 1)
    scale = np.exp2(byte - 127.0)
    codes = (blocks / scale).astype(np.float32).astype(dtype).astype(np.float64)
    return np.moveaxis((codes * scale).reshape(v.shape), -1, axis)


WIDE = False


def mx_kscale(k):
    if not WIDE:
        return np.ones(k)
    levels = np.array([10, -10, 5, -5, 0])
    if k % 512:
        return np.exp2(np.random.permutation(np.resize(levels, k // 32))).repeat(32)
    a = np.empty((k // 512, 16))
    for p in range(k // 512):
        a[p, :8] = np.random.permutation(np.resize(levels, 8))
        for g in range(8):
            far = levels[np.abs(levels - a[p, g]) >= 10]
            a[p, g + 8] = far[np.random.randint(len(far))]
    return np.exp2(a.ravel()).repeat(32)


BF16 = ml_dtypes.bfloat16


def bf(x):
    return np.asarray(x, np.float32).astype(BF16)


def f64(x):
    return np.asarray(x).astype(np.float64)


B, S, DIM, HEADS, DH = 1, 128, 512, 4, 128
HD = HEADS * DH
LN_EPS = 1e-5


def setup_inputs():
    s, t = mx_kscale(DIM), mx_kscale(HD)
    return {
        "x": bf(np.random.standard_normal((S, DIM)) + 0.5),
        "ln_w": bf((1.0 + 0.1 * np.random.standard_normal(DIM)) * s),
        "ln_b": bf(0.1 * np.random.standard_normal(DIM) * s),
        "W_c": bf(np.random.standard_normal((HD, DIM)) / np.sqrt(DIM) / s * t[:, None]),
        "b_c": bf(0.1 * np.random.standard_normal(HD) * t),
        "W_K": bf(np.random.standard_normal((HEADS, DH, DH, DH)) * 0.5 / np.sqrt(HD) / t.reshape(HEADS, 1, 1, DH)),
    }


def reference(x, ln_w, ln_b, W_c, b_c, W_K):
    x = f64(x)
    mu = x.mean(-1, keepdims=True)
    var = x.var(-1, keepdims=True)
    xn = (x - mu) / np.sqrt(var + LN_EPS) * f64(ln_w) + f64(ln_b)
    c = (mxq(xn, 1, "e4m3") @ mxq(f64(W_c), 1, "e4m3").T) + f64(b_c)
    wk = f64(W_K).transpose(0, 3, 1, 2).reshape(HD, DH * DH)
    return (mxq(c, 1, "e4m3") @ mxq(wk, 0, "e4m3")).reshape(S, DH, DH)

@@ -1,0 +1,250 @@
+from contextlib import ExitStack
+
+import concourse.mybir as mybir
+from concourse.masks import make_identity
+
+F32 = mybir.dt.float32
+BF16 = mybir.dt.bfloat16
+U32 = mybir.dt.uint32
+U8 = mybir.dt.uint8
+FP8X4 = mybir.dt.float8_e4m3fn_x4
+ALU = mybir.AluOpType
+ACT = mybir.ActivationFunctionType
+
+P = 128
+PACK = 4
+DIM = 512
+HEADS = 4
+DH = 128
+COLS = DH * DH
+LN_EPS = 1e-5
+
+WORDS = DH // 2
+HALF = WORDS // 2
+PASS_M = 4
+PASS_COLS = PASS_M * P
+ROUND = 2
+ROUND_M = ROUND * PASS_M
+BANK_M = 2
+CHUNK_ROUNDS = (1, 1, 2, 2, 2, 2, 2, 2, 1, 1)
+WAIT_FOR_W_C = 8
+WAIT_FOR_W_K = 2
+
+FLOPS = 2 * P * DIM * HEADS * DH + 2 * P * HEADS * DH * COLS
+
+
+def tile_trittentioncube_pa_kernel(tc, x, ln_w, ln_b, W_c, b_c, W_K, out):
+    nc = tc.nc
+    wk_cols = W_K.rearrange("n i j k -> n (i j) k")
+    out_cols = out.rearrange("r i j -> r (i j)")
+
+    with ExitStack() as ctx:
+        ctx.enter_context(tc.manual_schedule())
+        keep = ctx.enter_context(tc.tile_pool(name="keep", bufs=1))
+        raw_pool = ctx.enter_context(tc.tile_pool(name="raw", bufs=len(CHUNK_ROUNDS)))
+        runs_pool = ctx.enter_context(tc.tile_pool(name="runs", bufs=2))
+        grouped_pool = ctx.enter_context(tc.tile_pool(name="grouped", bufs=3))
+        mx_pool = ctx.enter_context(tc.tile_pool(name="mx", bufs=4))
+        flip_psum = ctx.enter_context(tc.psum_pool(name="flip_psum", bufs=6))
+        sum_psum = ctx.enter_context(tc.psum_pool(name="sum_psum", bufs=2))
+
+        zeros = keep.tile([P, PASS_COLS], BF16)
+        nc.vector.memset(zeros[:], 0.0)
+        ident = keep.tile([P, P], F32)
+        make_identity(nc, ident[:])
+        eps = keep.tile([P, 1], F32)
+        nc.vector.memset(eps[:], LN_EPS)
+
+        x_sb = keep.tile([P, DIM], BF16)
+        nc.sync.dma_start(out=x_sb[:], in_=x)
+        gain = keep.tile([P, PACK], BF16)
+        nc.scalar.dma_start(out=gain[:], in_=ln_w.rearrange("(p t) -> p t", t=PACK))
+        shift = keep.tile([P, PACK], BF16)
+        nc.scalar.dma_start(out=shift[:], in_=ln_b.rearrange("(p t) -> p t", t=PACK))
+        bias = keep.tile([P, PACK], BF16)
+        nc.scalar.dma_start(out=bias[:], in_=b_c.rearrange("(p t) -> p t", t=PACK))
+        wc_raw = keep.tile([P, PACK * DIM], BF16)
+        nc.sync.dma_start(out=wc_raw[:], in_=W_c.rearrange("(p t) d -> p (t d)", t=PACK))
+        raw_tiles = []
+        first_col = 0
+        for rounds in CHUNK_ROUNDS:
+            cols = rounds * ROUND * PASS_COLS
+            raw = raw_pool.tile([P, HEADS, (cols // P) * DH], BF16, tag="chunk")
+            nc.sync.dma_start(
+                out=raw[:],
+                in_=wk_cols[:, first_col : first_col + cols, :].rearrange("n (g m) k -> g n (m k)", g=P),
+            )
+            raw_tiles.append(raw)
+            first_col += cols
+
+        def raise_clock(count):
+            unread = sum_psum.tile([P, PASS_COLS], F32, tag="sums")
+            for i in range(count):
+                nc.tensor.matmul(
+                    out=unread[:], lhsT=zeros[:, 0:P], rhs=zeros[:], start=(i == 0), stop=(i == count - 1)
+                )
+
+        raise_clock(WAIT_FOR_W_C)
+
+        warm = keep.tile([P, 1], F32)
+        nc.scalar.activation(out=warm[:], in_=eps[:], func=ACT.Sqrt)
+
+        stats = keep.tile([P, 6], F32)
+        nc.vector.bn_stats(out=stats[:], in_=x_sb[:])
+        mean_var = keep.tile([P, 2], F32)
+        nc.vector.bn_aggr(out=mean_var[:], in_=stats[:])
+        std = keep.tile([P, 1], F32)
+        nc.scalar.activation(out=std[:], in_=mean_var[:, 1:2], func=ACT.Sqrt, bias=eps[:])
+        rstd = keep.tile([P, 1], F32)
+        nc.vector.reciprocal(out=rstd[:], in_=std[:])
+        xhat = keep.tile([P, PACK, P], F32)
+        nc.vector.tensor_scalar(
+            out=xhat[:], in0=x_sb[:].rearrange("r (q t) -> r t q", t=PACK),
+            scalar1=mean_var[:, 0:1], scalar2=rstd[:], op0=ALU.subtract, op1=ALU.mult,
+        )
+
+        def empty_bank(engine_copy, grouped_words, flip):
+            engine_copy(
+                out=grouped_words.rearrange("p (m g u) -> p m g u", m=BANK_M, u=2),
+                in_=flip[:].rearrange("p m u g -> p m g u"),
+            )
+
+        xhat_flip = flip_psum.tile([P, PACK, P], F32, tag="flip")
+        for t in range(PACK):
+            nc.tensor.transpose(xhat_flip[:, t, :], xhat[:, t, :], ident[:])
+        xn_scaled = keep.tile([P, P, PACK], F32)
+        nc.vector.tensor_tensor(
+            out=xn_scaled[:], in0=xhat_flip[:].rearrange("p t r -> p r t"),
+            in1=gain[:].unsqueeze(1).to_broadcast([P, P, PACK]), op=ALU.mult,
+        )
+        xn_grouped = keep.tile([P, P * PACK], BF16, align_bytes=64)
+        nc.vector.tensor_tensor(
+            out=xn_grouped[:].rearrange("p (r t) -> p r t", t=PACK), in0=xn_scaled[:],
+            in1=shift[:].unsqueeze(1).to_broadcast([P, P, PACK]), op=ALU.add,
+        )
+
+        wc_words = wc_raw[:].bitcast(F32)
+        wc_grouped = keep.tile([P, PACK * P * PACK], BF16, align_bytes=64)
+        for b in range(PACK // BANK_M):
+            flip = flip_psum.tile([P, BANK_M, 2, P], F32, tag="flip")
+            for mm in range(BANK_M):
+                row = (b * BANK_M + mm) * (DIM // 2)
+                for u in range(2):
+                    nc.tensor.transpose(flip[:, mm, u, :], wc_words[:, row + u : row + DIM // 2 : 2], ident[:])
+            empty_bank(
+                nc.scalar.copy,
+                wc_grouped[:].bitcast(F32)[:, b * PASS_COLS : (b + 1) * PASS_COLS],
+                flip,
+            )
+        xn_codes = keep.tile([P, P], U32, align_bytes=64)
+        xn_scales = keep.tile([P, P], U8, align_bytes=64)
+        nc.vector.quantize_mx(out=xn_codes[:].bitcast(FP8X4), scales=xn_scales[:], in_=xn_grouped[:])
+        wc_codes = keep.tile([P, PACK * P], U32, align_bytes=64)
+        wc_scales = keep.tile([P, PACK * P], U8, align_bytes=64)
+        nc.vector.quantize_mx(out=wc_codes[:].bitcast(FP8X4), scales=wc_scales[:], in_=wc_grouped[:])
+
+        places = []
+        for c, rounds in enumerate(CHUNK_ROUNDS):
+            for j in range(rounds):
+                places.append((c, j * ROUND_M))
+        runs_tiles = {}
+        grouped_tiles = {}
+        mx_tiles = {}
+        result_tiles = {}
+
+        def rearrange_round(i):
+            c, first_m = places[i]
+            words = raw_tiles[c][:].rearrange("p n f -> p (n f)").bitcast(F32).rearrange(
+                "p (n m w u) -> p u m n w", n=HEADS, w=HALF, u=2
+            )
+            runs = runs_pool.tile([P, 2, ROUND_M, P], F32)
+            for u in range(2):
+                nc.vector.tensor_copy(
+                    out=runs[:, u].rearrange("p m (n w) -> p m n w", n=HEADS),
+                    in_=words[:, u, first_m : first_m + ROUND_M],
+                )
+            runs_tiles[i] = runs
+
+        def flip_round(i):
+            runs = runs_tiles[i]
+            for s in range(ROUND):
+                grouped = grouped_pool.tile([P, PASS_COLS * PACK], BF16, align_bytes=64)
+                for b in range(PASS_M // BANK_M):
+                    flip = flip_psum.tile([P, BANK_M, 2, P], F32, tag="flip")
+                    for mm in range(BANK_M):
+                        for u in range(2):
+                            nc.tensor.transpose(
+                                flip[:, mm, u, :], runs[:, u, s * PASS_M + b * BANK_M + mm, :], ident[:]
+                            )
+                    empty_bank(
+                        nc.scalar.copy,
+                        grouped[:].bitcast(F32)[:, b * PASS_COLS : (b + 1) * PASS_COLS],
+                        flip,
+                    )
+                grouped_tiles[i * ROUND + s] = grouped
+
+        def quantise_pass(s):
+            codes = mx_pool.tile([P, PASS_COLS], U32, align_bytes=64)
+            scales = mx_pool.tile([P, PASS_COLS], U8, align_bytes=64)
+            nc.vector.quantize_mx(out=codes[:].bitcast(FP8X4), scales=scales[:], in_=grouped_tiles[s][:])
+            mx_tiles[s] = (codes, scales)
+
+        def multiply_pass(s, engine_copy):
+            codes, scales = mx_tiles[s]
+            sums = sum_psum.tile([P, PASS_COLS], F32, tag="sums")
+            nc.tensor.matmul_mx(
+                out=sums[:], lhsT=c_codes[:].bitcast(FP8X4), lhsT_scale=c_scales[:],
+                rhs=codes[:].bitcast(FP8X4), rhs_scale=scales[:], start=True, stop=True,
+            )
+            i, half = divmod(s, ROUND)
+            c, first_m = places[i]
+            first_m += half * PASS_M
+            chunk_m = CHUNK_ROUNDS[c] * ROUND_M
+            if first_m == 0:
+                result = raw_pool.tile([P, P, chunk_m], F32, tag="chunk")
+                result_tiles[c] = result
+            engine_copy(
+                out=result_tiles[c][:, :, first_m : first_m + PASS_M],
+                in_=sums[:].rearrange("r (m g) -> r g m", m=PASS_M),
+            )
+            if first_m + PASS_M == chunk_m:
+                col = sum(CHUNK_ROUNDS[:c]) * ROUND * PASS_COLS
+                nc.sync.dma_start(
+                    out=out_cols[:, col : col + P * chunk_m],
+                    in_=result_tiles[c][:].rearrange("r g m -> r (g m)"),
+                )
+
+        raise_clock(WAIT_FOR_W_K)
+        rearrange_round(0)
+        flip_round(0)
+        c_sums = sum_psum.tile([P, PACK, P], F32, tag="sums")
+        for t in range(PACK):
+            nc.tensor.matmul_mx(
+                out=c_sums[:, t, :],
+                lhsT=wc_codes[:, t * P : (t + 1) * P].bitcast(FP8X4),
+                lhsT_scale=wc_scales[:, t * P : (t + 1) * P],
+                rhs=xn_codes[:].bitcast(FP8X4), rhs_scale=xn_scales[:], start=True, stop=True,
+            )
+        rearrange_round(1)
+        c_grouped = keep.tile([P, P * PACK], BF16, align_bytes=64)
+        nc.vector.tensor_tensor(
+            out=c_grouped[:].rearrange("p (r t) -> p r t", t=PACK), in0=c_sums[:].rearrange("p t r -> p r t"),
+            in1=bias[:].unsqueeze(1).to_broadcast([P, P, PACK]), op=ALU.add,
+        )
+        quantise_pass(0)
+        c_codes = keep.tile([P, P], U32, align_bytes=64)
+        c_scales = keep.tile([P, P], U8, align_bytes=64)
+        nc.vector.quantize_mx(out=c_codes[:].bitcast(FP8X4), scales=c_scales[:], in_=c_grouped[:])
+        quantise_pass(1)
+
+        rounds = len(places)
+        for i in range(1, rounds):
+            flip_round(i)
+            if i + 1 < rounds:
+                rearrange_round(i + 1)
+            quantise_pass(2 * i)
+            multiply_pass(2 * i - 2, nc.vector.tensor_copy)
+            quantise_pass(2 * i + 1)
+            multiply_pass(2 * i - 1, nc.scalar.copy)
+        multiply_pass(2 * rounds - 2, nc.vector.tensor_copy)
+        multiply_pass(2 * rounds - 1, nc.scalar.copy)

@@ -27,6 +27,7 @@ ROUND = 2
 ROUND_M = ROUND * PASS_M
 BANK_M = 2
 CHUNK_ROUNDS = (1, 1, 2, 2, 2, 2, 2, 2, 1, 1)
+RESULTS = 7
 WAIT_FOR_W_C = 8
 WAIT_FOR_W_K = 2
 
@@ -41,7 +42,8 @@ def tile_trittentioncube_pa_kernel(tc, x, ln_w, ln_b, W_c, b_c, W_K, out):
     with ExitStack() as ctx:
         ctx.enter_context(tc.manual_schedule())
         keep = ctx.enter_context(tc.tile_pool(name="keep", bufs=1))
-        raw_pool = ctx.enter_context(tc.tile_pool(name="raw", bufs=len(CHUNK_ROUNDS)))
+        raw_pool = ctx.enter_context(tc.tile_pool(name="raw", bufs=1))
+        result_pool = ctx.enter_context(tc.tile_pool(name="result", bufs=1))
         runs_pool = ctx.enter_context(tc.tile_pool(name="runs", bufs=2))
         grouped_pool = ctx.enter_context(tc.tile_pool(name="grouped", bufs=3))
         mx_pool = ctx.enter_context(tc.tile_pool(name="mx", bufs=4))
@@ -69,7 +71,7 @@ def tile_trittentioncube_pa_kernel(tc, x, ln_w, ln_b, W_c, b_c, W_K, out):
         first_col = 0
         for rounds in CHUNK_ROUNDS:
             cols = rounds * ROUND * PASS_COLS
-            raw = raw_pool.tile([P, HEADS, (cols // P) * DH], BF16, tag="chunk")
+            raw = raw_pool.tile([P, HEADS, (cols // P) * DH], BF16, tag=f"raw{len(raw_tiles)}")
             nc.sync.dma_start(
                 out=raw[:],
                 in_=wk_cols[:, first_col : first_col + cols, :].rearrange("n (g m) k -> g n (m k)", g=P),
@@ -124,7 +126,7 @@ def tile_trittentioncube_pa_kernel(tc, x, ln_w, ln_b, W_c, b_c, W_K, out):
         )
 
         wc_words = wc_raw[:].bitcast(F32)
-        wc_grouped = keep.tile([P, PACK * P * PACK], BF16, align_bytes=64)
+        wc_grouped = grouped_pool.tile([P, PACK * P * PACK], BF16, align_bytes=64, tag="grouped")
         for b in range(PACK // BANK_M):
             flip = flip_psum.tile([P, BANK_M, 2, P], F32, tag="flip")
             for mm in range(BANK_M):
@@ -168,7 +170,7 @@ def tile_trittentioncube_pa_kernel(tc, x, ln_w, ln_b, W_c, b_c, W_K, out):
         def flip_round(i):
             runs = runs_tiles[i]
             for s in range(ROUND):
-                grouped = grouped_pool.tile([P, PASS_COLS * PACK], BF16, align_bytes=64)
+                grouped = grouped_pool.tile([P, PASS_COLS * PACK], BF16, align_bytes=64, tag="grouped")
                 for b in range(PASS_M // BANK_M):
                     flip = flip_psum.tile([P, BANK_M, 2, P], F32, tag="flip")
                     for mm in range(BANK_M):
@@ -201,7 +203,8 @@ def tile_trittentioncube_pa_kernel(tc, x, ln_w, ln_b, W_c, b_c, W_K, out):
             first_m += half * PASS_M
             chunk_m = CHUNK_ROUNDS[c] * ROUND_M
             if first_m == 0:
-                result = raw_pool.tile([P, P, chunk_m], F32, tag="chunk")
+                buffer = c if c < RESULTS else c - RESULTS + 2
+                result = result_pool.tile([P, P, chunk_m], F32, tag=f"result{buffer}")
                 result_tiles[c] = result
             engine_copy(
                 out=result_tiles[c][:, :, first_m : first_m + PASS_M],

@@ -24,12 +24,10 @@ HALF = WORDS // 2
 PASS_M = 4
 PASS_COLS = PASS_M * P
 ROUND = 2
-ROUND_M = ROUND * PASS_M
 BANK_M = 2
-CHUNK_ROUNDS = (1, 1, 2, 2, 2, 2, 2, 2, 1, 1)
-RESULTS = 7
-WAIT_FOR_W_C = 8
-WAIT_FOR_W_K = 2
+CHUNK_PASSES = (1, 1, 1, 1, 2, 2, 2, 2, 4, 4, 4, 4, 2, 1, 1)
+RESULT_BUFS = {1: 4, 2: 4, 4: 3}
+WARM_UP = 6
 
 FLOPS = 2 * P * DIM * HEADS * DH + 2 * P * HEADS * DH * COLS
 
@@ -43,15 +41,18 @@ def tile_trittentioncube_pa_kernel(tc, x, ln_w, ln_b, W_c, b_c, W_K, out):
         ctx.enter_context(tc.manual_schedule())
         keep = ctx.enter_context(tc.tile_pool(name="keep", bufs=1))
         raw_pool = ctx.enter_context(tc.tile_pool(name="raw", bufs=1))
-        result_pool = ctx.enter_context(tc.tile_pool(name="result", bufs=1))
-        runs_pool = ctx.enter_context(tc.tile_pool(name="runs", bufs=2))
-        grouped_pool = ctx.enter_context(tc.tile_pool(name="grouped", bufs=3))
+        result_pools = {
+            passes: ctx.enter_context(tc.tile_pool(name=f"result{passes}", bufs=bufs))
+            for passes, bufs in RESULT_BUFS.items()
+        }
+        runs_pool = ctx.enter_context(tc.tile_pool(name="runs", bufs=3))
+        grouped_pool = ctx.enter_context(tc.tile_pool(name="grouped", bufs=4))
         mx_pool = ctx.enter_context(tc.tile_pool(name="mx", bufs=4))
-        flip_psum = ctx.enter_context(tc.psum_pool(name="flip_psum", bufs=6))
-        sum_psum = ctx.enter_context(tc.psum_pool(name="sum_psum", bufs=2))
+        flip_psum = ctx.enter_context(tc.psum_pool(name="flip_psum", bufs=4))
+        sum_psum = ctx.enter_context(tc.psum_pool(name="sum_psum", bufs=4))
 
         zeros = keep.tile([P, PASS_COLS], BF16)
-        nc.vector.memset(zeros[:], 0.0)
+        nc.gpsimd.memset(zeros[:], 0.0)
         ident = keep.tile([P, P], F32)
         make_identity(nc, ident[:])
         eps = keep.tile([P, 1], F32)
@@ -59,25 +60,30 @@ def tile_trittentioncube_pa_kernel(tc, x, ln_w, ln_b, W_c, b_c, W_K, out):
 
         x_sb = keep.tile([P, DIM], BF16)
         nc.sync.dma_start(out=x_sb[:], in_=x)
-        gain = keep.tile([P, PACK], BF16)
-        nc.scalar.dma_start(out=gain[:], in_=ln_w.rearrange("(p t) -> p t", t=PACK))
-        shift = keep.tile([P, PACK], BF16)
-        nc.scalar.dma_start(out=shift[:], in_=ln_b.rearrange("(p t) -> p t", t=PACK))
-        bias = keep.tile([P, PACK], BF16)
-        nc.scalar.dma_start(out=bias[:], in_=b_c.rearrange("(p t) -> p t", t=PACK))
-        wc_raw = keep.tile([P, PACK * DIM], BF16)
-        nc.sync.dma_start(out=wc_raw[:], in_=W_c.rearrange("(p t) d -> p (t d)", t=PACK))
         raw_tiles = []
+        chunk_views = []
         first_col = 0
-        for rounds in CHUNK_ROUNDS:
-            cols = rounds * ROUND * PASS_COLS
+        for passes in CHUNK_PASSES:
+            cols = passes * PASS_COLS
             raw = raw_pool.tile([P, HEADS, (cols // P) * DH], BF16, tag=f"raw{len(raw_tiles)}")
-            nc.sync.dma_start(
-                out=raw[:],
-                in_=wk_cols[:, first_col : first_col + cols, :].rearrange("n (g m) k -> g n (m k)", g=P),
-            )
             raw_tiles.append(raw)
+            chunk_views.append(
+                wk_cols[:, first_col : first_col + cols, :].rearrange("n (g m) k -> g n (m k)", g=P)
+            )
             first_col += cols
+        wc_raw = keep.tile([P, PACK * DIM], BF16)
+        vecs = []
+        for v in range(3):
+            vec_sb = keep.tile([P, PACK], BF16, tag=f"vec{v}")
+            vecs.append(vec_sb)
+        bias = vecs[2]
+        for c in range(len(CHUNK_PASSES)):
+            nc.sync.dma_start(out=raw_tiles[c][:], in_=chunk_views[c])
+            if c == 0:
+                for vec_sb, vec in zip(vecs, (ln_w, ln_b, b_c)):
+                    nc.sync.dma_start(out=vec_sb[:], in_=vec.rearrange("(p t) -> p t", t=PACK))
+            if c == 1:
+                nc.sync.dma_start(out=wc_raw[:], in_=W_c.rearrange("(p t) d -> p (t d)", t=PACK))
 
         def raise_clock(count):
             unread = sum_psum.tile([P, PASS_COLS], F32, tag="sums")
@@ -86,7 +92,7 @@ def tile_trittentioncube_pa_kernel(tc, x, ln_w, ln_b, W_c, b_c, W_K, out):
                     out=unread[:], lhsT=zeros[:, 0:P], rhs=zeros[:], start=(i == 0), stop=(i == count - 1)
                 )
 
-        raise_clock(WAIT_FOR_W_C)
+        raise_clock(WARM_UP)
 
         warm = keep.tile([P, 1], F32)
         nc.scalar.activation(out=warm[:], in_=eps[:], func=ACT.Sqrt)
@@ -105,85 +111,50 @@ def tile_trittentioncube_pa_kernel(tc, x, ln_w, ln_b, W_c, b_c, W_K, out):
             scalar1=mean_var[:, 0:1], scalar2=rstd[:], op0=ALU.subtract, op1=ALU.mult,
         )
 
+        gain = keep.tile([P, PACK], F32)
+        nc.vector.tensor_copy(out=gain[:], in_=vecs[0][:])
+        shift = keep.tile([P, PACK], F32)
+        nc.vector.tensor_copy(out=shift[:], in_=vecs[1][:])
+
         def empty_bank(engine_copy, grouped_words, flip):
             engine_copy(
                 out=grouped_words.rearrange("p (m g u) -> p m g u", m=BANK_M, u=2),
                 in_=flip[:].rearrange("p m u g -> p m g u"),
             )
 
-        xhat_flip = flip_psum.tile([P, PACK, P], F32, tag="flip")
-        for t in range(PACK):
-            nc.tensor.transpose(xhat_flip[:, t, :], xhat[:, t, :], ident[:])
-        xn_scaled = keep.tile([P, P, PACK], F32)
-        nc.vector.tensor_tensor(
-            out=xn_scaled[:], in0=xhat_flip[:].rearrange("p t r -> p r t"),
-            in1=gain[:].unsqueeze(1).to_broadcast([P, P, PACK]), op=ALU.mult,
-        )
-        xn_grouped = keep.tile([P, P * PACK], BF16, align_bytes=64)
-        nc.vector.tensor_tensor(
-            out=xn_grouped[:].rearrange("p (r t) -> p r t", t=PACK), in0=xn_scaled[:],
-            in1=shift[:].unsqueeze(1).to_broadcast([P, P, PACK]), op=ALU.add,
-        )
-
-        wc_words = wc_raw[:].bitcast(F32)
-        wc_grouped = grouped_pool.tile([P, PACK * P * PACK], BF16, align_bytes=64, tag="grouped")
-        for b in range(PACK // BANK_M):
-            flip = flip_psum.tile([P, BANK_M, 2, P], F32, tag="flip")
-            for mm in range(BANK_M):
-                row = (b * BANK_M + mm) * (DIM // 2)
-                for u in range(2):
-                    nc.tensor.transpose(flip[:, mm, u, :], wc_words[:, row + u : row + DIM // 2 : 2], ident[:])
-            empty_bank(
-                nc.scalar.copy,
-                wc_grouped[:].bitcast(F32)[:, b * PASS_COLS : (b + 1) * PASS_COLS],
-                flip,
-            )
-        xn_codes = keep.tile([P, P], U32, align_bytes=64)
-        xn_scales = keep.tile([P, P], U8, align_bytes=64)
-        nc.vector.quantize_mx(out=xn_codes[:].bitcast(FP8X4), scales=xn_scales[:], in_=xn_grouped[:])
-        wc_codes = keep.tile([P, PACK * P], U32, align_bytes=64)
-        wc_scales = keep.tile([P, PACK * P], U8, align_bytes=64)
-        nc.vector.quantize_mx(out=wc_codes[:].bitcast(FP8X4), scales=wc_scales[:], in_=wc_grouped[:])
-
         places = []
-        for c, rounds in enumerate(CHUNK_ROUNDS):
-            for j in range(rounds):
-                places.append((c, j * ROUND_M))
+        for c, chunk_passes in enumerate(CHUNK_PASSES):
+            for j in range(chunk_passes):
+                places.append((c, j * PASS_M))
         runs_tiles = {}
         grouped_tiles = {}
         mx_tiles = {}
         result_tiles = {}
 
-        def rearrange_round(i):
-            c, first_m = places[i]
+        def rearrange_pass(s):
+            c, first_m = places[s]
             words = raw_tiles[c][:].rearrange("p n f -> p (n f)").bitcast(F32).rearrange(
                 "p (n m w u) -> p u m n w", n=HEADS, w=HALF, u=2
             )
-            runs = runs_pool.tile([P, 2, ROUND_M, P], F32)
-            for u in range(2):
-                nc.vector.tensor_copy(
-                    out=runs[:, u].rearrange("p m (n w) -> p m n w", n=HEADS),
-                    in_=words[:, u, first_m : first_m + ROUND_M],
-                )
-            runs_tiles[i] = runs
+            runs = runs_pool.tile([P, 2, PASS_M, P], F32)
+            nc.vector.tensor_copy(
+                out=runs[:].rearrange("p u m (n w) -> p u m n w", n=HEADS),
+                in_=words[:, :, first_m : first_m + PASS_M],
+            )
+            runs_tiles[s] = runs
 
-        def flip_round(i):
-            runs = runs_tiles[i]
-            for s in range(ROUND):
-                grouped = grouped_pool.tile([P, PASS_COLS * PACK], BF16, align_bytes=64, tag="grouped")
-                for b in range(PASS_M // BANK_M):
-                    flip = flip_psum.tile([P, BANK_M, 2, P], F32, tag="flip")
-                    for mm in range(BANK_M):
-                        for u in range(2):
-                            nc.tensor.transpose(
-                                flip[:, mm, u, :], runs[:, u, s * PASS_M + b * BANK_M + mm, :], ident[:]
-                            )
-                    empty_bank(
-                        nc.scalar.copy,
-                        grouped[:].bitcast(F32)[:, b * PASS_COLS : (b + 1) * PASS_COLS],
-                        flip,
-                    )
-                grouped_tiles[i * ROUND + s] = grouped
+        def flip_pass(s):
+            runs = runs_tiles[s]
+            grouped = grouped_pool.tile([P, PASS_COLS * PACK], BF16, align_bytes=64, tag="grouped")
+            for b in range(PASS_M // BANK_M):
+                flip = flip_psum.tile([P, BANK_M, 2, P], F32, tag="flip")
+                for mm in range(BANK_M):
+                    for u in range(2):
+                        nc.tensor.transpose(flip[:, mm, u, :], runs[:, u, b * BANK_M + mm, :], ident[:])
+                empty_bank(
+                    nc.scalar.copy, grouped[:].bitcast(F32)[:, b * PASS_COLS : (b + 1) * PASS_COLS], flip
+                )
+            grouped_tiles[s] = grouped
 
         def quantise_pass(s):
             codes = mx_pool.tile([P, PASS_COLS], U32, align_bytes=64)
@@ -198,28 +169,64 @@ def tile_trittentioncube_pa_kernel(tc, x, ln_w, ln_b, W_c, b_c, W_K, out):
                 out=sums[:], lhsT=c_codes[:].bitcast(FP8X4), lhsT_scale=c_scales[:],
                 rhs=codes[:].bitcast(FP8X4), rhs_scale=scales[:], start=True, stop=True,
             )
-            i, half = divmod(s, ROUND)
-            c, first_m = places[i]
-            first_m += half * PASS_M
-            chunk_m = CHUNK_ROUNDS[c] * ROUND_M
+            c, first_m = places[s]
+            chunk_m = CHUNK_PASSES[c] * PASS_M
             if first_m == 0:
-                buffer = c if c < RESULTS else c - RESULTS + 2
-                result = result_pool.tile([P, P, chunk_m], F32, tag=f"result{buffer}")
+                result = result_pools[CHUNK_PASSES[c]].tile([P, P, chunk_m], F32)
                 result_tiles[c] = result
             engine_copy(
                 out=result_tiles[c][:, :, first_m : first_m + PASS_M],
                 in_=sums[:].rearrange("r (m g) -> r g m", m=PASS_M),
             )
             if first_m + PASS_M == chunk_m:
-                col = sum(CHUNK_ROUNDS[:c]) * ROUND * PASS_COLS
+                col = sum(CHUNK_PASSES[:c]) * PASS_COLS
                 nc.sync.dma_start(
                     out=out_cols[:, col : col + P * chunk_m],
                     in_=result_tiles[c][:].rearrange("r g m -> r (g m)"),
                 )
 
-        raise_clock(WAIT_FOR_W_K)
-        rearrange_round(0)
-        flip_round(0)
+        xhat_flip = flip_psum.tile([P, PACK, P], F32, tag="flip")
+        for t in range(PACK):
+            nc.tensor.transpose(xhat_flip[:, t, :], xhat[:, t, :], ident[:])
+        rearrange_pass(0)
+        xn = keep.tile([P, PACK, P], BF16)
+        for t in range(PACK):
+            nc.scalar.activation(
+                out=xn[:, t, :], in_=xhat_flip[:, t, :], func=ACT.Identity,
+                scale=gain[:, t : t + 1], bias=shift[:, t : t + 1],
+            )
+        flip_pass(0)
+        rearrange_pass(1)
+        flip_pass(1)
+        xn_grouped = keep.tile([P, P * PACK], BF16, align_bytes=64)
+        nc.vector.tensor_copy(
+            out=xn_grouped[:].rearrange("p (r t) -> p r t", t=PACK), in_=xn[:].rearrange("p t r -> p r t")
+        )
+
+        wc_words = wc_raw[:].bitcast(F32)
+        wc_grouped = grouped_pool.tile([P, PACK * P * PACK], BF16, align_bytes=64, tag="grouped")
+        for b in range(PACK // BANK_M):
+            flip = flip_psum.tile([P, BANK_M, 2, P], F32, tag="flip")
+            for mm in range(BANK_M):
+                row = (b * BANK_M + mm) * (DIM // 2)
+                for u in range(2):
+                    nc.tensor.transpose(flip[:, mm, u, :], wc_words[:, row + u : row + DIM // 2 : 2], ident[:])
+            empty_bank(
+                nc.scalar.copy, wc_grouped[:].bitcast(F32)[:, b * PASS_COLS : (b + 1) * PASS_COLS], flip
+            )
+        xn_codes = keep.tile([P, P], U32, align_bytes=64)
+        xn_scales = keep.tile([P, P], U8, align_bytes=64)
+        nc.vector.quantize_mx(out=xn_codes[:].bitcast(FP8X4), scales=xn_scales[:], in_=xn_grouped[:])
+        rearrange_pass(2)
+        flip_pass(2)
+        quantise_pass(0)
+        rearrange_pass(3)
+        flip_pass(3)
+        quantise_pass(1)
+        wc_codes = keep.tile([P, PACK * P], U32, align_bytes=64)
+        wc_scales = keep.tile([P, PACK * P], U8, align_bytes=64)
+        nc.vector.quantize_mx(out=wc_codes[:].bitcast(FP8X4), scales=wc_scales[:], in_=wc_grouped[:])
+
         c_sums = sum_psum.tile([P, PACK, P], F32, tag="sums")
         for t in range(PACK):
             nc.tensor.matmul_mx(
@@ -228,26 +235,28 @@ def tile_trittentioncube_pa_kernel(tc, x, ln_w, ln_b, W_c, b_c, W_K, out):
                 lhsT_scale=wc_scales[:, t * P : (t + 1) * P],
                 rhs=xn_codes[:].bitcast(FP8X4), rhs_scale=xn_scales[:], start=True, stop=True,
             )
-        rearrange_round(1)
+        rearrange_pass(4)
         c_grouped = keep.tile([P, P * PACK], BF16, align_bytes=64)
         nc.vector.tensor_tensor(
             out=c_grouped[:].rearrange("p (r t) -> p r t", t=PACK), in0=c_sums[:].rearrange("p t r -> p r t"),
             in1=bias[:].unsqueeze(1).to_broadcast([P, P, PACK]), op=ALU.add,
         )
-        quantise_pass(0)
+        quantise_pass(2)
         c_codes = keep.tile([P, P], U32, align_bytes=64)
         c_scales = keep.tile([P, P], U8, align_bytes=64)
         nc.vector.quantize_mx(out=c_codes[:].bitcast(FP8X4), scales=c_scales[:], in_=c_grouped[:])
-        quantise_pass(1)
+        rearrange_pass(5)
 
-        rounds = len(places)
-        for i in range(1, rounds):
-            flip_round(i)
-            if i + 1 < rounds:
-                rearrange_round(i + 1)
-            quantise_pass(2 * i)
-            multiply_pass(2 * i - 2, nc.vector.tensor_copy)
-            quantise_pass(2 * i + 1)
-            multiply_pass(2 * i - 1, nc.scalar.copy)
-        multiply_pass(2 * rounds - 2, nc.vector.tensor_copy)
-        multiply_pass(2 * rounds - 1, nc.scalar.copy)
+        total = len(places)
+        for s in range(0, total, ROUND):
+            for ahead in (s + 4, s + 5):
+                if ahead < total:
+                    flip_pass(ahead)
+            for ahead in (s + 6, s + 7):
+                if ahead < total:
+                    rearrange_pass(ahead)
+            for j in range(ROUND):
+                on_vector = j == 0 and s % (8 * ROUND) != 4 * ROUND
+                if s + 3 + j < total:
+                    quantise_pass(s + 3 + j)
+                multiply_pass(s + j, nc.vector.tensor_copy if on_vector else nc.scalar.copy)

@@ -25,8 +25,8 @@ PASS_M = 4
 PASS_COLS = PASS_M * P
 ROUND = 2
 BANK_M = 2
-CHUNK_PASSES = (1, 1, 1, 1, 2, 2, 2, 2, 4, 4, 4, 4, 2, 1, 1)
-RESULT_BUFS = {1: 4, 2: 4, 4: 3}
+CHUNK_PASSES = (2, 2, 2, 2, 2, 4, 4, 4, 4, 2, 2, 2)
+RESULT_BUFS = {2: 5, 4: 3}
 WARM_UP = 6
 
 FLOPS = 2 * P * DIM * HEADS * DH + 2 * P * HEADS * DH * COLS

@@ -134,12 +134,12 @@ def tile_trittentioncube_pa_kernel(tc, x, ln_w, ln_b, W_c, b_c, W_K, out):
         def rearrange_pass(s):
             c, first_m = places[s]
             words = raw_tiles[c][:].rearrange("p n f -> p (n f)").bitcast(F32).rearrange(
-                "p (n m w u) -> p u m n w", n=HEADS, w=HALF, u=2
+                "p (n m w u) -> p m u n w", n=HEADS, w=HALF, u=2
             )
-            runs = runs_pool.tile([P, 2, PASS_M, P], F32)
+            runs = runs_pool.tile([P, PASS_M, 2, P], F32)
             nc.vector.tensor_copy(
-                out=runs[:].rearrange("p u m (n w) -> p u m n w", n=HEADS),
-                in_=words[:, :, first_m : first_m + PASS_M],
+                out=runs[:].rearrange("p m u (n w) -> p m u n w", n=HEADS),
+                in_=words[:, first_m : first_m + PASS_M],
             )
             runs_tiles[s] = runs
 
@@ -150,7 +150,7 @@ def tile_trittentioncube_pa_kernel(tc, x, ln_w, ln_b, W_c, b_c, W_K, out):
                 flip = flip_psum.tile([P, BANK_M, 2, P], F32, tag="flip")
                 for mm in range(BANK_M):
                     for u in range(2):
-                        nc.tensor.transpose(flip[:, mm, u, :], runs[:, u, b * BANK_M + mm, :], ident[:])
+                        nc.tensor.transpose(flip[:, mm, u, :], runs[:, b * BANK_M + mm, u, :], ident[:])
                 empty_bank(
                     nc.scalar.copy, grouped[:].bitcast(F32)[:, b * PASS_COLS : (b + 1) * PASS_COLS], flip
                 )

@@ -256,7 +256,7 @@ def tile_trittentioncube_pa_kernel(tc, x, ln_w, ln_b, W_c, b_c, W_K, out):
                 if ahead < total:
                     rearrange_pass(ahead)
             for j in range(ROUND):
-                on_vector = j == 0 and s % (8 * ROUND) != 4 * ROUND
+                on_vector = j == 0 and s % (4 * ROUND) != 2 * ROUND
                 if s + 3 + j < total:
                     quantise_pass(s + 3 + j)
                 multiply_pass(s + j, nc.vector.tensor_copy if on_vector else nc.scalar.copy)

@@ -26,7 +26,8 @@ PASS_COLS = PASS_M * P
 ROUND = 2
 BANK_M = 2
 CHUNK_PASSES = (2, 2, 2, 2, 2, 4, 4, 4, 4, 2, 2, 2)
-RESULT_BUFS = {2: 5, 4: 3}
+RESULT_CHUNKS = ((0, 1, 2, 3, 4), (5, 6), (7,), (8,), (9, 10, 11))
+WHOLE_TILES = 2
 WARM_UP = 6
 
 FLOPS = 2 * P * DIM * HEADS * DH + 2 * P * HEADS * DH * COLS
@@ -41,10 +42,7 @@ def tile_trittentioncube_pa_kernel(tc, x, ln_w, ln_b, W_c, b_c, W_K, out):
         ctx.enter_context(tc.manual_schedule())
         keep = ctx.enter_context(tc.tile_pool(name="keep", bufs=1))
         raw_pool = ctx.enter_context(tc.tile_pool(name="raw", bufs=1))
-        result_pools = {
-            passes: ctx.enter_context(tc.tile_pool(name=f"result{passes}", bufs=bufs))
-            for passes, bufs in RESULT_BUFS.items()
-        }
+        result_pool = ctx.enter_context(tc.tile_pool(name="result", bufs=1))
         runs_pool = ctx.enter_context(tc.tile_pool(name="runs", bufs=3))
         grouped_pool = ctx.enter_context(tc.tile_pool(name="grouped", bufs=4))
         mx_pool = ctx.enter_context(tc.tile_pool(name="mx", bufs=4))
@@ -171,18 +169,27 @@ def tile_trittentioncube_pa_kernel(tc, x, ln_w, ln_b, W_c, b_c, W_K, out):
             )
             c, first_m = places[s]
             chunk_m = CHUNK_PASSES[c] * PASS_M
-            if first_m == 0:
-                result = result_pools[CHUNK_PASSES[c]].tile([P, P, chunk_m], F32)
-                result_tiles[c] = result
+            tile_number = [c in chunks for chunks in RESULT_CHUNKS].index(True)
+            chunks = RESULT_CHUNKS[tile_number]
+            tile_col = sum(CHUNK_PASSES[: chunks[0]]) * PASS_COLS
+            col = sum(CHUNK_PASSES[:c]) * PASS_COLS
+            end_col = col + P * chunk_m
+            if first_m == 0 and c == chunks[0]:
+                cols = sum(CHUNK_PASSES[k] for k in chunks) * PASS_COLS
+                tag = f"result{tile_number % (len(RESULT_CHUNKS) - 1)}"
+                result = result_pool.tile([P, cols], F32, tag=tag)
+                result_tiles[tile_number] = result
+            result = result_tiles[tile_number]
             engine_copy(
-                out=result_tiles[c][:, :, first_m : first_m + PASS_M],
+                out=result[:, col - tile_col : end_col - tile_col].rearrange("r (g m) -> r g m", g=P)[
+                    :, :, first_m : first_m + PASS_M
+                ],
                 in_=sums[:].rearrange("r (m g) -> r g m", m=PASS_M),
             )
-            if first_m + PASS_M == chunk_m:
-                col = sum(CHUNK_PASSES[:c]) * PASS_COLS
+            if first_m + PASS_M == chunk_m and (tile_number >= WHOLE_TILES or c == chunks[-1]):
+                start_col = tile_col if tile_number < WHOLE_TILES else col
                 nc.sync.dma_start(
-                    out=out_cols[:, col : col + P * chunk_m],
-                    in_=result_tiles[c][:].rearrange("r g m -> r (g m)"),
+                    out=out_cols[:, start_col:end_col], in_=result[:, start_col - tile_col : end_col - tile_col]
                 )
 
         xhat_flip = flip_psum.tile([P, PACK, P], F32, tag="flip")

@@ -26,6 +26,7 @@ PASS_COLS = PASS_M * P
 ROUND = 2
 BANK_M = 2
 CHUNK_PASSES = (2, 2, 2, 2, 2, 4, 4, 4, 4, 2, 2, 2)
+RAW_TILES = 9
 RESULT_CHUNKS = ((0, 1, 2, 3, 4), (5, 6), (7,), (8,), (9, 10, 11))
 WHOLE_TILES = 2
 WARM_UP = 6
@@ -43,8 +44,8 @@ def tile_trittentioncube_pa_kernel(tc, x, ln_w, ln_b, W_c, b_c, W_K, out):
         keep = ctx.enter_context(tc.tile_pool(name="keep", bufs=1))
         raw_pool = ctx.enter_context(tc.tile_pool(name="raw", bufs=1))
         result_pool = ctx.enter_context(tc.tile_pool(name="result", bufs=1))
-        runs_pool = ctx.enter_context(tc.tile_pool(name="runs", bufs=3))
-        grouped_pool = ctx.enter_context(tc.tile_pool(name="grouped", bufs=4))
+        runs_pool = ctx.enter_context(tc.tile_pool(name="runs", bufs=4))
+        grouped_pool = ctx.enter_context(tc.tile_pool(name="grouped", bufs=5))
         mx_pool = ctx.enter_context(tc.tile_pool(name="mx", bufs=4))
         flip_psum = ctx.enter_context(tc.psum_pool(name="flip_psum", bufs=4))
         sum_psum = ctx.enter_context(tc.psum_pool(name="sum_psum", bufs=4))
@@ -59,24 +60,25 @@ def tile_trittentioncube_pa_kernel(tc, x, ln_w, ln_b, W_c, b_c, W_K, out):
         x_sb = keep.tile([P, DIM], BF16)
         nc.sync.dma_start(out=x_sb[:], in_=x)
         raw_tiles = []
-        chunk_views = []
-        first_col = 0
-        for passes in CHUNK_PASSES:
-            cols = passes * PASS_COLS
-            raw = raw_pool.tile([P, HEADS, (cols // P) * DH], BF16, tag=f"raw{len(raw_tiles)}")
-            raw_tiles.append(raw)
-            chunk_views.append(
-                wk_cols[:, first_col : first_col + cols, :].rearrange("n (g m) k -> g n (m k)", g=P)
+
+        def load_chunk(c):
+            cols = CHUNK_PASSES[c] * PASS_COLS
+            first_col = sum(CHUNK_PASSES[:c]) * PASS_COLS
+            raw = raw_pool.tile([P, HEADS, (cols // P) * DH], BF16, tag=f"raw{c % RAW_TILES}")
+            nc.sync.dma_start(
+                out=raw[:],
+                in_=wk_cols[:, first_col : first_col + cols, :].rearrange("n (g m) k -> g n (m k)", g=P),
             )
-            first_col += cols
+            raw_tiles.append(raw)
+
         wc_raw = keep.tile([P, PACK * DIM], BF16)
         vecs = []
         for v in range(3):
             vec_sb = keep.tile([P, PACK], BF16, tag=f"vec{v}")
             vecs.append(vec_sb)
         bias = vecs[2]
-        for c in range(len(CHUNK_PASSES)):
-            nc.sync.dma_start(out=raw_tiles[c][:], in_=chunk_views[c])
+        for c in range(RAW_TILES):
+            load_chunk(c)
             if c == 0:
                 for vec_sb, vec in zip(vecs, (ln_w, ln_b, b_c)):
                     nc.sync.dma_start(out=vec_sb[:], in_=vec.rearrange("(p t) -> p t", t=PACK))
@@ -176,8 +178,7 @@ def tile_trittentioncube_pa_kernel(tc, x, ln_w, ln_b, W_c, b_c, W_K, out):
             end_col = col + P * chunk_m
             if first_m == 0 and c == chunks[0]:
                 cols = sum(CHUNK_PASSES[k] for k in chunks) * PASS_COLS
-                tag = f"result{tile_number % (len(RESULT_CHUNKS) - 1)}"
-                result = result_pool.tile([P, cols], F32, tag=tag)
+                result = result_pool.tile([P, cols], F32, tag=f"result{tile_number}")
                 result_tiles[tile_number] = result
             result = result_tiles[tile_number]
             engine_copy(
@@ -253,6 +254,8 @@ def tile_trittentioncube_pa_kernel(tc, x, ln_w, ln_b, W_c, b_c, W_K, out):
         c_scales = keep.tile([P, P], U8, align_bytes=64)
         nc.vector.quantize_mx(out=c_codes[:].bitcast(FP8X4), scales=c_scales[:], in_=c_grouped[:])
         rearrange_pass(5)
+        for c in range(RAW_TILES, len(CHUNK_PASSES)):
+            load_chunk(c)
 
         total = len(places)
         for s in range(0, total, ROUND):

from contextlib import ExitStack

import concourse.mybir as mybir
from concourse.masks import make_identity

F32 = mybir.dt.float32
BF16 = mybir.dt.bfloat16
U32 = mybir.dt.uint32
U8 = mybir.dt.uint8
FP8X4 = mybir.dt.float8_e4m3fn_x4
ALU = mybir.AluOpType
ACT = mybir.ActivationFunctionType

P = 128
PACK = 4
DIM = 512
HEADS = 4
DH = 128
COLS = DH * DH
LN_EPS = 1e-5

WORDS = DH // 2
HALF = WORDS // 2
PASS_M = 4
PASS_COLS = PASS_M * P
ROUND = 2
BANK_M = 2
CHUNK_PASSES = (2, 2, 2, 2, 2, 4, 4, 4, 4, 2, 2, 2)
RAW_TILES = 9
RESULT_CHUNKS = ((0, 1, 2, 3, 4), (5, 6), (7,), (8,), (9, 10, 11))
WHOLE_TILES = 2
WARM_UP = 6

FLOPS = 2 * P * DIM * HEADS * DH + 2 * P * HEADS * DH * COLS


def tile_trittentioncube_pa_kernel(tc, x, ln_w, ln_b, W_c, b_c, W_K, out):
    nc = tc.nc
    wk_cols = W_K.rearrange("n i j k -> n (i j) k")
    out_cols = out.rearrange("r i j -> r (i j)")

    with ExitStack() as ctx:
        ctx.enter_context(tc.manual_schedule())
        keep = ctx.enter_context(tc.tile_pool(name="keep", bufs=1))
        raw_pool = ctx.enter_context(tc.tile_pool(name="raw", bufs=1))
        result_pool = ctx.enter_context(tc.tile_pool(name="result", bufs=1))
        runs_pool = ctx.enter_context(tc.tile_pool(name="runs", bufs=4))
        grouped_pool = ctx.enter_context(tc.tile_pool(name="grouped", bufs=5))
        mx_pool = ctx.enter_context(tc.tile_pool(name="mx", bufs=4))
        flip_psum = ctx.enter_context(tc.psum_pool(name="flip_psum", bufs=4))
        sum_psum = ctx.enter_context(tc.psum_pool(name="sum_psum", bufs=4))

        zeros = keep.tile([P, PASS_COLS], BF16)
        nc.gpsimd.memset(zeros[:], 0.0)
        ident = keep.tile([P, P], F32)
        make_identity(nc, ident[:])
        eps = keep.tile([P, 1], F32)
        nc.vector.memset(eps[:], LN_EPS)

        x_sb = keep.tile([P, DIM], BF16)
        nc.sync.dma_start(out=x_sb[:], in_=x)
        raw_tiles = []

        def load_chunk(c):
            cols = CHUNK_PASSES[c] * PASS_COLS
            first_col = sum(CHUNK_PASSES[:c]) * PASS_COLS
            raw = raw_pool.tile([P, HEADS, (cols // P) * DH], BF16, tag=f"raw{c % RAW_TILES}")
            nc.sync.dma_start(
                out=raw[:],
                in_=wk_cols[:, first_col : first_col + cols, :].rearrange("n (g m) k -> g n (m k)", g=P),
            )
            raw_tiles.append(raw)

        wc_raw = keep.tile([P, PACK * DIM], BF16)
        vecs = []
        for v in range(3):
            vec_sb = keep.tile([P, PACK], BF16, tag=f"vec{v}")
            vecs.append(vec_sb)
        bias = vecs[2]
        for c in range(RAW_TILES):
            load_chunk(c)
            if c == 0:
                for vec_sb, vec in zip(vecs, (ln_w, ln_b, b_c)):
                    nc.sync.dma_start(out=vec_sb[:], in_=vec.rearrange("(p t) -> p t", t=PACK))
            if c == 1:
                nc.sync.dma_start(out=wc_raw[:], in_=W_c.rearrange("(p t) d -> p (t d)", t=PACK))

        def raise_clock(count):
            unread = sum_psum.tile([P, PASS_COLS], F32, tag="sums")
            for i in range(count):
                nc.tensor.matmul(
                    out=unread[:], lhsT=zeros[:, 0:P], rhs=zeros[:], start=(i == 0), stop=(i == count - 1)
                )

        raise_clock(WARM_UP)

        warm = keep.tile([P, 1], F32)
        nc.scalar.activation(out=warm[:], in_=eps[:], func=ACT.Sqrt)

        stats = keep.tile([P, 6], F32)
        nc.vector.bn_stats(out=stats[:], in_=x_sb[:])
        mean_var = keep.tile([P, 2], F32)
        nc.vector.bn_aggr(out=mean_var[:], in_=stats[:])
        std = keep.tile([P, 1], F32)
        nc.scalar.activation(out=std[:], in_=mean_var[:, 1:2], func=ACT.Sqrt, bias=eps[:])
        rstd = keep.tile([P, 1], F32)
        nc.vector.reciprocal(out=rstd[:], in_=std[:])
        xhat = keep.tile([P, PACK, P], F32)
        nc.vector.tensor_scalar(
            out=xhat[:], in0=x_sb[:].rearrange("r (q t) -> r t q", t=PACK),
            scalar1=mean_var[:, 0:1], scalar2=rstd[:], op0=ALU.subtract, op1=ALU.mult,
        )

        gain = keep.tile([P, PACK], F32)
        nc.vector.tensor_copy(out=gain[:], in_=vecs[0][:])
        shift = keep.tile([P, PACK], F32)
        nc.vector.tensor_copy(out=shift[:], in_=vecs[1][:])

        def empty_bank(engine_copy, grouped_words, flip):
            engine_copy(
                out=grouped_words.rearrange("p (m g u) -> p m g u", m=BANK_M, u=2),
                in_=flip[:].rearrange("p m u g -> p m g u"),
            )

        places = []
        for c, chunk_passes in enumerate(CHUNK_PASSES):
            for j in range(chunk_passes):
                places.append((c, j * PASS_M))
        runs_tiles = {}
        grouped_tiles = {}
        mx_tiles = {}
        result_tiles = {}

        def rearrange_pass(s):
            c, first_m = places[s]
            words = raw_tiles[c][:].rearrange("p n f -> p (n f)").bitcast(F32).rearrange(
                "p (n m w u) -> p m u n w", n=HEADS, w=HALF, u=2
            )
            runs = runs_pool.tile([P, PASS_M, 2, P], F32)
            nc.vector.tensor_copy(
                out=runs[:].rearrange("p m u (n w) -> p m u n w", n=HEADS),
                in_=words[:, first_m : first_m + PASS_M],
            )
            runs_tiles[s] = runs

        def flip_pass(s):
            runs = runs_tiles[s]
            grouped = grouped_pool.tile([P, PASS_COLS * PACK], BF16, align_bytes=64, tag="grouped")
            for b in range(PASS_M // BANK_M):
                flip = flip_psum.tile([P, BANK_M, 2, P], F32, tag="flip")
                for mm in range(BANK_M):
                    for u in range(2):
                        nc.tensor.transpose(flip[:, mm, u, :], runs[:, b * BANK_M + mm, u, :], ident[:])
                empty_bank(
                    nc.scalar.copy, grouped[:].bitcast(F32)[:, b * PASS_COLS : (b + 1) * PASS_COLS], flip
                )
            grouped_tiles[s] = grouped

        def quantise_pass(s):
            codes = mx_pool.tile([P, PASS_COLS], U32, align_bytes=64)
            scales = mx_pool.tile([P, PASS_COLS], U8, align_bytes=64)
            nc.vector.quantize_mx(out=codes[:].bitcast(FP8X4), scales=scales[:], in_=grouped_tiles[s][:])
            mx_tiles[s] = (codes, scales)

        def multiply_pass(s, engine_copy):
            codes, scales = mx_tiles[s]
            sums = sum_psum.tile([P, PASS_COLS], F32, tag="sums")
            nc.tensor.matmul_mx(
                out=sums[:], lhsT=c_codes[:].bitcast(FP8X4), lhsT_scale=c_scales[:],
                rhs=codes[:].bitcast(FP8X4), rhs_scale=scales[:], start=True, stop=True,
            )
            c, first_m = places[s]
            chunk_m = CHUNK_PASSES[c] * PASS_M
            tile_number = [c in chunks for chunks in RESULT_CHUNKS].index(True)
            chunks = RESULT_CHUNKS[tile_number]
            tile_col = sum(CHUNK_PASSES[: chunks[0]]) * PASS_COLS
            col = sum(CHUNK_PASSES[:c]) * PASS_COLS
            end_col = col + P * chunk_m
            if first_m == 0 and c == chunks[0]:
                cols = sum(CHUNK_PASSES[k] for k in chunks) * PASS_COLS
                result = result_pool.tile([P, cols], F32, tag=f"result{tile_number}")
                result_tiles[tile_number] = result
            result = result_tiles[tile_number]
            engine_copy(
                out=result[:, col - tile_col : end_col - tile_col].rearrange("r (g m) -> r g m", g=P)[
                    :, :, first_m : first_m + PASS_M
                ],
                in_=sums[:].rearrange("r (m g) -> r g m", m=PASS_M),
            )
            if first_m + PASS_M == chunk_m and (tile_number >= WHOLE_TILES or c == chunks[-1]):
                start_col = tile_col if tile_number < WHOLE_TILES else col
                nc.sync.dma_start(
                    out=out_cols[:, start_col:end_col], in_=result[:, start_col - tile_col : end_col - tile_col]
                )

        xhat_flip = flip_psum.tile([P, PACK, P], F32, tag="flip")
        for t in range(PACK):
            nc.tensor.transpose(xhat_flip[:, t, :], xhat[:, t, :], ident[:])
        rearrange_pass(0)
        xn = keep.tile([P, PACK, P], BF16)
        for t in range(PACK):
            nc.scalar.activation(
                out=xn[:, t, :], in_=xhat_flip[:, t, :], func=ACT.Identity,
                scale=gain[:, t : t + 1], bias=shift[:, t : t + 1],
            )
        flip_pass(0)
        rearrange_pass(1)
        flip_pass(1)
        xn_grouped = keep.tile([P, P * PACK], BF16, align_bytes=64)
        nc.vector.tensor_copy(
            out=xn_grouped[:].rearrange("p (r t) -> p r t", t=PACK), in_=xn[:].rearrange("p t r -> p r t")
        )

        wc_words = wc_raw[:].bitcast(F32)
        wc_grouped = grouped_pool.tile([P, PACK * P * PACK], BF16, align_bytes=64, tag="grouped")
        for b in range(PACK // BANK_M):
            flip = flip_psum.tile([P, BANK_M, 2, P], F32, tag="flip")
            for mm in range(BANK_M):
                row = (b * BANK_M + mm) * (DIM // 2)
                for u in range(2):
                    nc.tensor.transpose(flip[:, mm, u, :], wc_words[:, row + u : row + DIM // 2 : 2], ident[:])
            empty_bank(
                nc.scalar.copy, wc_grouped[:].bitcast(F32)[:, b * PASS_COLS : (b + 1) * PASS_COLS], flip
            )
        xn_codes = keep.tile([P, P], U32, align_bytes=64)
        xn_scales = keep.tile([P, P], U8, align_bytes=64)
        nc.vector.quantize_mx(out=xn_codes[:].bitcast(FP8X4), scales=xn_scales[:], in_=xn_grouped[:])
        rearrange_pass(2)
        flip_pass(2)
        quantise_pass(0)
        rearrange_pass(3)
        flip_pass(3)
        quantise_pass(1)
        wc_codes = keep.tile([P, PACK * P], U32, align_bytes=64)
        wc_scales = keep.tile([P, PACK * P], U8, align_bytes=64)
        nc.vector.quantize_mx(out=wc_codes[:].bitcast(FP8X4), scales=wc_scales[:], in_=wc_grouped[:])

        c_sums = sum_psum.tile([P, PACK, P], F32, tag="sums")
        for t in range(PACK):
            nc.tensor.matmul_mx(
                out=c_sums[:, t, :],
                lhsT=wc_codes[:, t * P : (t + 1) * P].bitcast(FP8X4),
                lhsT_scale=wc_scales[:, t * P : (t + 1) * P],
                rhs=xn_codes[:].bitcast(FP8X4), rhs_scale=xn_scales[:], start=True, stop=True,
            )
        rearrange_pass(4)
        c_grouped = keep.tile([P, P * PACK], BF16, align_bytes=64)
        nc.vector.tensor_tensor(
            out=c_grouped[:].rearrange("p (r t) -> p r t", t=PACK), in0=c_sums[:].rearrange("p t r -> p r t"),
            in1=bias[:].unsqueeze(1).to_broadcast([P, P, PACK]), op=ALU.add,
        )
        quantise_pass(2)
        c_codes = keep.tile([P, P], U32, align_bytes=64)
        c_scales = keep.tile([P, P], U8, align_bytes=64)
        nc.vector.quantize_mx(out=c_codes[:].bitcast(FP8X4), scales=c_scales[:], in_=c_grouped[:])
        rearrange_pass(5)
        for c in range(RAW_TILES, len(CHUNK_PASSES)):
            load_chunk(c)

        total = len(places)
        for s in range(0, total, ROUND):
            for ahead in (s + 4, s + 5):
                if ahead < total:
                    flip_pass(ahead)
            for ahead in (s + 6, s + 7):
                if ahead < total:
                    rearrange_pass(ahead)
            for j in range(ROUND):
                on_vector = j == 0 and s % (4 * ROUND) != 2 * ROUND
                if s + 3 + j < total:
                    quantise_pass(s + 3 + j)
                multiply_pass(s + j, nc.vector.tensor_copy if on_vector else nc.scalar.copy)
